import numpy as np
import ml_dtypes


def mxq(x, axis, fmt="e4m3"):
    dtype, down = {"e4m3": (ml_dtypes.float8_e4m3fn, 7), "e5m2": (ml_dtypes.float8_e5m2, 14)}[fmt]
    v = np.moveaxis(np.asarray(x, np.float32).astype(ml_dtypes.bfloat16).astype(np.float64), axis, -1)
    blocks = v.reshape(v.shape[:-1] + (-1, 32))
    amax = np.abs(blocks).max(-1, keepdims=True)
    byte = np.maximum(np.where(amax > 0, np.frexp(amax)[1] - 1 + 127, 0) - down, 1)
    scale = np.exp2(byte - 127.0)
    codes = (blocks / scale).astype(np.float32).astype(dtype).astype(np.float64)
    return np.moveaxis((codes * scale).reshape(v.shape), -1, axis)


WIDE = False


def mx_kscale(k):
    if not WIDE:
        return np.ones(k)
    levels = np.array([10, -10, 5, -5, 0])
    if k % 512:
        return np.exp2(np.random.permutation(np.resize(levels, k // 32))).repeat(32)
    a = np.empty((k // 512, 16))
    for p in range(k // 512):
        a[p, :8] = np.random.permutation(np.resize(levels, 8))
        for g in range(8):
            far = levels[np.abs(levels - a[p, g]) >= 10]
            a[p, g + 8] = far[np.random.randint(len(far))]
    return np.exp2(a.ravel()).repeat(32)


BF16 = ml_dtypes.bfloat16


def bf(x):
    return np.asarray(x, np.float32).astype(BF16)


def f64(x):
    return np.asarray(x).astype(np.float64)


T, B, D, H, HD, A = 512, 1, 1024, 16, 128, 128
HH = H * HD
HA = H * A
N = HH + HH + HA + HA
EPS = 1e-5
QK = 1.5


def layer_norm(x, w, b):
    mu = x.mean(-1, keepdims=True)
    var = np.square(x - mu).mean(-1, keepdims=True)
    return (x - mu) * (1.0 / np.sqrt(var + EPS)) * w + b


def setup_inputs():
    s = mx_kscale(D)
    col = np.concatenate([np.ones(HH + HH), QK * np.ones(HA + HA)])
    return {"src": bf(np.random.standard_normal((T, B, D))),
            "ln1_w": bf((1.0 + 0.1 * np.random.standard_normal(D)) * s),
            "ln1_b": bf(0.1 * np.random.standard_normal(D) * s),
            "w_uvqk": bf(np.random.standard_normal((D, N)) * col / np.sqrt(D) / s[:, None]),
            "b_uvqk": bf(0.1 * np.random.standard_normal(N))}


def reference(src, ln1_w, ln1_b, w_uvqk, b_uvqk):
    src_norm = layer_norm(f64(src), f64(ln1_w), f64(ln1_b))
    return (mxq(src_norm, 2, "e4m3") @ mxq(f64(w_uvqk), 0, "e4m3")) + f64(b_uvqk)

@@ -1,0 +1,319 @@
+from contextlib import ExitStack
+
+import concourse.mybir as mybir
+from concourse.masks import make_identity
+
+F32 = mybir.dt.float32
+BF16 = mybir.dt.bfloat16
+U32 = mybir.dt.uint32
+U8 = mybir.dt.uint8
+FP8X4 = mybir.dt.float8_e4m3fn_x4
+ALU = mybir.AluOpType
+ACT = mybir.ActivationFunctionType
+
+P = 128
+PACK = 4
+T = 512
+D = 1024
+N = 8192
+EPS = 1e-5
+PASSES = D // (P * PACK)
+GROUPS = PASSES * PACK
+TOKEN_TILES = T // P
+N_TILE = 512
+PARTS = N // N_TILE
+LOAD_COLS = 2048
+PARTS_PER_LOAD = LOAD_COLS // N_TILE
+LOADS = (N // LOAD_COLS) * PASSES
+LOADS_AHEAD = 6
+STORE_COLS = 1024
+STORES = N // STORE_COLS
+PARTS_PER_STORE = STORE_COLS // N_TILE
+RUN = 4
+GPSIMD_EVERY = 2
+BN_FMAX = 512
+BN_STATS_DIM = 6
+BN_AGGR_DIM = 2
+
+FLOPS = 2 * T * D * N
+
+
+def regroup(engine_copy, grouped, rows):
+    engine_copy(
+        out=grouped.rearrange("p (q i) t -> p q t i", i=RUN),
+        in_=rows.rearrange("p t (q i) -> p q t i", i=RUN),
+    )
+
+
+def tile_stulayer_pa_kernel(tc, src, ln1_w, ln1_b, w_uvqk, b_uvqk, out):
+    nc = tc.nc
+    src_rows = src.rearrange("t b d -> (t b) d")
+    out_rows = out.rearrange("t b n -> (t b) n")
+    w_view = w_uvqk.rearrange("(c p t) n -> p c t n", c=PASSES, t=PACK, p=P)
+
+    with ExitStack() as ctx:
+        keep = ctx.enter_context(tc.tile_pool(name="keep", bufs=1))
+        raw_pool = ctx.enter_context(tc.tile_pool(name="raw", bufs=LOADS_AHEAD))
+        grouped_pool = ctx.enter_context(tc.tile_pool(name="grouped", bufs=3))
+        code_pool = ctx.enter_context(tc.tile_pool(name="codes", bufs=4))
+        psum = ctx.enter_context(tc.psum_pool(name="psum", bufs=8))
+        ctx.enter_context(tc.manual_schedule())
+
+        raw = []
+
+        def load_w(number, piece, pieces):
+            if piece == 0:
+                raw_tile = raw_pool.tile([P, PACK, LOAD_COLS], BF16, name="raw_tile", tag="raw")
+                raw.append(raw_tile)
+            width = LOAD_COLS // pieces
+            local = piece * width
+            first = (number // PASSES) * LOAD_COLS + local
+            nc.sync.dma_start(
+                out=raw[number][:, :, local : local + width],
+                in_=w_view[:, number % PASSES, :, first : first + width],
+            )
+
+        with tc.tile_pool(name="head", bufs=1) as head:
+
+            ln_rows = keep.tile([P, P * PACK], BF16)
+            nc.vector.memset(ln_rows[:], 0.0)
+            bias_rows = keep.tile([P, N_TILE], BF16)
+            nc.vector.memset(bias_rows[:], 0.0)
+            eps_col = keep.tile([P, 1], F32)
+            nc.vector.memset(eps_col[:], EPS)
+            x_tiles = []
+            for i in range(TOKEN_TILES):
+                x_i = head.tile([P, D], BF16, name="x%d" % i)
+                nc.sync.dma_start(out=x_i[:], in_=src_rows[i * P : (i + 1) * P, :])
+                x_tiles.append(x_i)
+                if i == 0:
+                    nc.sync.dma_start(
+                        out=bias_rows[0:PARTS, :], in_=b_uvqk.rearrange("(r n) -> r n", n=N_TILE)
+                    )
+                    nc.sync.dma_start(
+                        out=ln_rows[0:PASSES, :],
+                        in_=ln1_w.rearrange("(c f) -> c f", c=PASSES),
+                    )
+                    nc.sync.dma_start(
+                        out=ln_rows[PASSES : 2 * PASSES, :],
+                        in_=ln1_b.rearrange("(c f) -> c f", c=PASSES),
+                    )
+            for piece in range(2):
+                for number in range(PASSES):
+                    load_w(number, piece, 2)
+            for number in range(PASSES, LOADS_AHEAD):
+                load_w(number, 0, 1)
+
+
+            ident_bf = keep.tile([P, P], BF16)
+            make_identity(nc, ident_bf[:])
+            ident = keep.tile([P, P], F32)
+            make_identity(nc, ident[:])
+
+            ln_cols_ps = psum.tile([P, PACK, P], BF16, tag="bank")
+            for t in range(PACK):
+                nc.tensor.transpose(ln_cols_ps[:, t, :], ln_rows[:, t : P * PACK : PACK], ident_bf[:])
+            gain_shift = keep.tile([P, PACK, 2 * PASSES], F32)
+            nc.vector.tensor_copy(out=gain_shift[:], in_=ln_cols_ps[:, :, 0 : 2 * PASSES])
+
+            bias_all = keep.tile([P, N], BF16)
+
+            def spread_bias(pair):
+                bias_ps = psum.tile([P, 2 * N_TILE], BF16, tag="bank")
+                for half in range(2):
+                    r = 2 * pair + half
+                    nc.tensor.matmul(
+                        out=bias_ps[:, half * N_TILE : (half + 1) * N_TILE],
+                        lhsT=ident_bf[:, r : r + 1].to_broadcast([P, P]),
+                        rhs=bias_rows[:],
+                        start=True,
+                        stop=True,
+                    )
+                nc.scalar.copy(
+                    out=bias_all[:, pair * 2 * N_TILE : (pair + 1) * 2 * N_TILE], in_=bias_ps[:]
+                )
+
+            stats = keep.tile([P, TOKEN_TILES, D // BN_FMAX, BN_STATS_DIM], F32)
+            mean_var = keep.tile([P, TOKEN_TILES, BN_AGGR_DIM], F32)
+            std = keep.tile([P, TOKEN_TILES], F32)
+            rstd = keep.tile([P, TOKEN_TILES], F32)
+            neg_mean = keep.tile([P, TOKEN_TILES], F32)
+            xhat_tiles = []
+
+            def statistics(i):
+                for h in range(D // BN_FMAX):
+                    nc.vector.bn_stats(
+                        out=stats[:, i, h, :], in_=x_tiles[i][:, h * BN_FMAX : (h + 1) * BN_FMAX]
+                    )
+                nc.vector.bn_aggr(
+                    out=mean_var[:, i, :], in_=stats[:, i, :, :].rearrange("p h s -> p (h s)")
+                )
+                nc.scalar.activation(
+                    out=std[:, i : i + 1], in_=mean_var[:, i, 1:2], func=ACT.Sqrt,
+                    bias=eps_col[:, 0:1], scale=1.0,
+                )
+
+            def normalise(i):
+                nc.vector.reciprocal(out=rstd[:, i : i + 1], in_=std[:, i : i + 1])
+                nc.vector.tensor_scalar(
+                    out=neg_mean[:, i : i + 1], in0=mean_var[:, i, 0:1], scalar1=-1.0, scalar2=None,
+                    op0=ALU.mult,
+                )
+                xhat_i = head.tile([P, GROUPS, P], F32, name="xhat%d" % i)
+                engine = nc.vector if i == TOKEN_TILES - 1 else nc.gpsimd
+                engine.tensor_scalar(
+                    out=xhat_i[:].rearrange("p (c t) q -> p c t q", c=PASSES),
+                    in0=x_tiles[i][:].rearrange("p (c q t) -> p c t q", c=PASSES, t=PACK),
+                    scalar1=neg_mean[:, i : i + 1],
+                    scalar2=rstd[:, i : i + 1],
+                    op0=ALU.add,
+                    op1=ALU.mult,
+                )
+                xhat_tiles.append(xhat_i)
+
+            pairs_per_tile = PARTS // 2 // TOKEN_TILES
+            for i in range(TOKEN_TILES):
+                statistics(i)
+                for pair in range(i * pairs_per_tile, (i + 1) * pairs_per_tile):
+                    spread_bias(pair)
+                if i >= 1:
+                    normalise(i - 1)
+            normalise(TOKEN_TILES - 1)
+
+            xt_banks = []
+            for g in range(GROUPS):
+                xt_g = psum.tile([P, T], F32, name="xt%d" % g, tag="bank")
+                xt_banks.append(xt_g)
+            for i in range(TOKEN_TILES):
+                for g in range(GROUPS):
+                    nc.tensor.transpose(
+                        xt_banks[g][:, i * P : (i + 1) * P],
+                        xhat_tiles[i][:, g, :],
+                        ident[:],
+                    )
+
+            grouped = {}
+            codes = {}
+            accs = {}
+            stages = {}
+
+            def gpsimd_copy(out, in_):
+                nc.gpsimd.tensor_scalar(
+                    out=out, in0=in_, scalar1=1.0, scalar2=0.0, op0=ALU.mult, op1=ALU.add
+                )
+
+            def regroup_part(part):
+                w_grouped = grouped_pool.tile([P, PASSES, N_TILE, PACK], BF16, align_bytes=64)
+                first = (part % PARTS_PER_LOAD) * N_TILE
+                for c in range(PASSES):
+                    number = (part // PARTS_PER_LOAD) * PASSES + c
+                    if c == PASSES - 1 and part % GPSIMD_EVERY == 0:
+                        copy = gpsimd_copy
+                    else:
+                        copy = nc.scalar.copy
+                    regroup(copy, w_grouped[:, c, :, :], raw[number][:, :, first : first + N_TILE])
+                grouped[part] = w_grouped
+
+            def quantise_part(part):
+                w_codes = code_pool.tile([P, PASSES * N_TILE], U32, align_bytes=64)
+                w_scales = code_pool.tile([P, PASSES * N_TILE], U8, align_bytes=64)
+                nc.vector.quantize_mx(
+                    out=w_codes[:].bitcast(FP8X4),
+                    scales=w_scales[:],
+                    in_=grouped[part][:].rearrange("p c n t -> p (c n t)"),
+                )
+                codes[part] = (w_codes, w_scales)
+
+            def multiply(part):
+                for i in range(TOKEN_TILES):
+                    acc_i = psum.tile([P, N_TILE], F32, name="acc_i", tag="bank")
+                    accs[(part, i)] = acc_i
+                w_codes, w_scales = codes[part]
+                for c in range(PASSES):
+                    columns = slice(c * N_TILE, (c + 1) * N_TILE)
+                    for i in range(TOKEN_TILES):
+                        tokens = slice(c * T + i * P, c * T + (i + 1) * P)
+                        nc.tensor.matmul_mx(
+                            out=accs[(part, i)][:],
+                            lhsT=x_codes[:, tokens].bitcast(FP8X4),
+                            lhsT_scale=x_scales[:, tokens],
+                            rhs=w_codes[:, columns].bitcast(FP8X4),
+                            rhs_scale=w_scales[:, columns],
+                            start=(c == 0),
+                            stop=(c == PASSES - 1),
+                        )
+
+            def add_bias_and_store(part):
+                store = part // PARTS_PER_STORE
+                local = (part % PARTS_PER_STORE) * N_TILE
+                first = part * N_TILE
+                for i in range(TOKEN_TILES):
+                    if local == 0:
+                        stage_i = stage_pool.tile([P, STORE_COLS], F32, name="stage_i", tag="stage")
+                        stages[(store, i)] = stage_i
+                    stage = stages[(store, i)]
+                    token_rows = slice(i * P, (i + 1) * P)
+                    nc.vector.tensor_tensor(
+                        out=stage[:, local : local + N_TILE],
+                        in0=accs[(part, i)][:],
+                        in1=bias_all[:, first : first + N_TILE],
+                        op=ALU.add,
+                    )
+                    if store == STORES - 1:
+                        nc.sync.dma_start(
+                            out=out_rows[token_rows, first : first + N_TILE],
+                            in_=stage[:, local : local + N_TILE],
+                        )
+                    elif local + N_TILE == STORE_COLS:
+                        nc.sync.dma_start(
+                            out=out_rows[token_rows, store * STORE_COLS : (store + 1) * STORE_COLS],
+                            in_=stage[:],
+                        )
+
+            regroup_part(0)
+
+            x_norm = head.tile([P, GROUPS, T], BF16)
+            for g in range(GROUPS):
+                c, t = divmod(g, PACK)
+                gain = gain_shift[:, t, c : c + 1]
+                shift = gain_shift[:, t, PASSES + c : PASSES + c + 1]
+                if g % 2 == 0:
+                    nc.scalar.activation(
+                        out=x_norm[:, g, :], in_=xt_banks[g][:], func=ACT.Identity,
+                        scale=gain, bias=shift,
+                    )
+                else:
+                    nc.vector.tensor_scalar(
+                        out=x_norm[:, g, :], in0=xt_banks[g][:], scalar1=gain, scalar2=shift,
+                        op0=ALU.mult, op1=ALU.add,
+                    )
+
+            x_grouped = head.tile([P, PASSES, T, PACK], BF16, align_bytes=64)
+            for c in range(PASSES):
+                regroup(
+                    nc.vector.tensor_copy,
+                    x_grouped[:, c, :, :],
+                    x_norm[:, c * PACK : (c + 1) * PACK, :],
+                )
+            quantise_part(0)
+            x_codes = keep.tile([P, PASSES * T], U32, align_bytes=64)
+            x_scales = keep.tile([P, PASSES * T], U8, align_bytes=64)
+            nc.vector.quantize_mx(
+                out=x_codes[:].bitcast(FP8X4),
+                scales=x_scales[:],
+                in_=x_grouped[:].rearrange("p c n t -> p (c n t)"),
+            )
+
+        stage_pool = ctx.enter_context(tc.tile_pool(name="stage", bufs=3 * TOKEN_TILES))
+
+        for part in range(PARTS + 1):
+            if 1 <= part < PARTS:
+                regroup_part(part)
+                quantise_part(part)
+            if part < PARTS:
+                multiply(part)
+            if part >= 1:
+                add_bias_and_store(part - 1)
+                loads_read = PASSES * (min(part + 1, PARTS) // PARTS_PER_LOAD)
+                if part % PARTS_PER_STORE == 0 and len(raw) < min(LOADS, LOADS_AHEAD + loads_read):
+                    load_w(len(raw), 0, 1)

@@ -20,17 +20,19 @@ EPS = 1e-5
 PASSES = D // (P * PACK)
 GROUPS = PASSES * PACK
 TOKEN_TILES = T // P
+HALVES = 2
+TILES_PER_HALF = TOKEN_TILES // HALVES
+T_HALF = T // HALVES
+BANKS = 8
 N_TILE = 512
 PARTS = N // N_TILE
-LOAD_COLS = 2048
-PARTS_PER_LOAD = LOAD_COLS // N_TILE
-LOADS = (N // LOAD_COLS) * PASSES
-LOADS_AHEAD = 6
+LOAD_PARTS = (1, 3, 4, 8)
 STORE_COLS = 1024
 STORES = N // STORE_COLS
 PARTS_PER_STORE = STORE_COLS // N_TILE
+STAGES = 13
 RUN = 4
-GPSIMD_EVERY = 2
+GPSIMD_COLS = 256
 BN_FMAX = 512
 BN_STATS_DIM = 6
 BN_AGGR_DIM = 2
@@ -53,25 +55,10 @@ def tile_stulayer_pa_kernel(tc, src, ln1_w, ln1_b, w_uvqk, b_uvqk, out):
 
     with ExitStack() as ctx:
         keep = ctx.enter_context(tc.tile_pool(name="keep", bufs=1))
-        raw_pool = ctx.enter_context(tc.tile_pool(name="raw", bufs=LOADS_AHEAD))
-        grouped_pool = ctx.enter_context(tc.tile_pool(name="grouped", bufs=3))
-        code_pool = ctx.enter_context(tc.tile_pool(name="codes", bufs=4))
-        psum = ctx.enter_context(tc.psum_pool(name="psum", bufs=8))
+        grouped_pool = ctx.enter_context(tc.tile_pool(name="grouped", bufs=2))
+        code_pool = ctx.enter_context(tc.tile_pool(name="codes", bufs=3))
+        psum = ctx.enter_context(tc.psum_pool(name="psum", bufs=1))
         ctx.enter_context(tc.manual_schedule())
-
-        raw = []
-
-        def load_w(number, piece, pieces):
-            if piece == 0:
-                raw_tile = raw_pool.tile([P, PACK, LOAD_COLS], BF16, name="raw_tile", tag="raw")
-                raw.append(raw_tile)
-            width = LOAD_COLS // pieces
-            local = piece * width
-            first = (number // PASSES) * LOAD_COLS + local
-            nc.sync.dma_start(
-                out=raw[number][:, :, local : local + width],
-                in_=w_view[:, number % PASSES, :, first : first + width],
-            )
 
         with tc.tile_pool(name="head", bufs=1) as head:
 
@@ -91,35 +78,49 @@ def tile_stulayer_pa_kernel(tc, src, ln1_w, ln1_b, w_uvqk, b_uvqk, out):
                         out=bias_rows[0:PARTS, :], in_=b_uvqk.rearrange("(r n) -> r n", n=N_TILE)
                     )
                     nc.sync.dma_start(
-                        out=ln_rows[0:PASSES, :],
-                        in_=ln1_w.rearrange("(c f) -> c f", c=PASSES),
+                        out=ln_rows[0:PASSES, :], in_=ln1_w.rearrange("(c f) -> c f", c=PASSES)
                     )
                     nc.sync.dma_start(
                         out=ln_rows[PASSES : 2 * PASSES, :],
                         in_=ln1_b.rearrange("(c f) -> c f", c=PASSES),
                     )
-            for piece in range(2):
-                for number in range(PASSES):
-                    load_w(number, piece, 2)
-            for number in range(PASSES, LOADS_AHEAD):
-                load_w(number, 0, 1)
-
+            raw = []
+            first = 0
+            for parts in LOAD_PARTS:
+                tiles = []
+                for c in range(PASSES):
+                    raw_tile = keep.tile(
+                        [P, PACK, parts * N_TILE], BF16, name="raw%d_%d" % (first, c)
+                    )
+                    nc.sync.dma_start(
+                        out=raw_tile[:], in_=w_view[:, c, :, first : first + parts * N_TILE]
+                    )
+                    tiles.append(raw_tile)
+                for j in range(parts):
+                    raw.append([tile[:, :, j * N_TILE : (j + 1) * N_TILE] for tile in tiles])
+                first += parts * N_TILE
 
             ident_bf = keep.tile([P, P], BF16)
             make_identity(nc, ident_bf[:])
             ident = keep.tile([P, P], F32)
             make_identity(nc, ident[:])
 
-            ln_cols_ps = psum.tile([P, PACK, P], BF16, tag="bank")
-            for t in range(PACK):
-                nc.tensor.transpose(ln_cols_ps[:, t, :], ln_rows[:, t : P * PACK : PACK], ident_bf[:])
             gain_shift = keep.tile([P, PACK, 2 * PASSES], F32)
-            nc.vector.tensor_copy(out=gain_shift[:], in_=ln_cols_ps[:, :, 0 : 2 * PASSES])
+
+            def turn_gain_and_shift():
+                ln_cols_ps = psum.tile([P, PACK, P], BF16, tag="bank0")
+                for t in range(PACK):
+                    nc.tensor.transpose(
+                        ln_cols_ps[:, t, :], ln_rows[:, t : P * PACK : PACK], ident_bf[:]
+                    )
+                nc.vector.tensor_copy(out=gain_shift[:], in_=ln_cols_ps[:, :, 0 : 2 * PASSES])
 
             bias_all = keep.tile([P, N], BF16)
 
             def spread_bias(pair):
-                bias_ps = psum.tile([P, 2 * N_TILE], BF16, tag="bank")
+                bias_ps = psum.tile(
+                    [P, 2 * N_TILE], BF16, name="bias_ps", tag="bank%d" % (BANKS // 2 + pair % (BANKS // 2))
+                )
                 for half in range(2):
                     r = 2 * pair + half
                     nc.tensor.matmul(
@@ -152,15 +153,14 @@ def tile_stulayer_pa_kernel(tc, src, ln1_w, ln1_b, w_uvqk, b_uvqk, out):
                     out=std[:, i : i + 1], in_=mean_var[:, i, 1:2], func=ACT.Sqrt,
                     bias=eps_col[:, 0:1], scale=1.0,
                 )
-
-            def normalise(i):
-                nc.vector.reciprocal(out=rstd[:, i : i + 1], in_=std[:, i : i + 1])
                 nc.vector.tensor_scalar(
                     out=neg_mean[:, i : i + 1], in0=mean_var[:, i, 0:1], scalar1=-1.0, scalar2=None,
                     op0=ALU.mult,
                 )
+
+            def normalise(i, engine):
+                nc.vector.reciprocal(out=rstd[:, i : i + 1], in_=std[:, i : i + 1])
                 xhat_i = head.tile([P, GROUPS, P], F32, name="xhat%d" % i)
-                engine = nc.vector if i == TOKEN_TILES - 1 else nc.gpsimd
                 engine.tensor_scalar(
                     out=xhat_i[:].rearrange("p (c t) q -> p c t q", c=PASSES),
                     in0=x_tiles[i][:].rearrange("p (c q t) -> p c t q", c=PASSES, t=PACK),
@@ -171,47 +171,75 @@ def tile_stulayer_pa_kernel(tc, src, ln1_w, ln1_b, w_uvqk, b_uvqk, out):
                 )
                 xhat_tiles.append(xhat_i)
 
-            pairs_per_tile = PARTS // 2 // TOKEN_TILES
-            for i in range(TOKEN_TILES):
-                statistics(i)
-                for pair in range(i * pairs_per_tile, (i + 1) * pairs_per_tile):
-                    spread_bias(pair)
-                if i >= 1:
-                    normalise(i - 1)
-            normalise(TOKEN_TILES - 1)
+            xt_banks = {}
 
-            xt_banks = []
-            for g in range(GROUPS):
-                xt_g = psum.tile([P, T], F32, name="xt%d" % g, tag="bank")
-                xt_banks.append(xt_g)
-            for i in range(TOKEN_TILES):
+            def turn_tokens(i):
+                h, local = divmod(i, TILES_PER_HALF)
                 for g in range(GROUPS):
+                    if local == 0 and g % 2 == 0:
+                        xt_banks[(h, g // 2)] = psum.tile(
+                            [P, 2, T_HALF], F32, name="xt", tag="bank%d" % (h * (BANKS // 2) + g // 2)
+                        )
                     nc.tensor.transpose(
-                        xt_banks[g][:, i * P : (i + 1) * P],
+                        xt_banks[(h, g // 2)][:, g % 2, local * P : (local + 1) * P],
                         xhat_tiles[i][:, g, :],
                         ident[:],
                     )
+
+            x_norm = head.tile([P, HALVES, GROUPS, T_HALF], BF16)
+
+            def gain_and_shift(h, g, on_scalar):
+                c, t = divmod(g, PACK)
+                gain = gain_shift[:, t, c : c + 1]
+                shift = gain_shift[:, t, PASSES + c : PASSES + c + 1]
+                if on_scalar:
+                    nc.scalar.activation(
+                        out=x_norm[:, h, g, :], in_=xt_banks[(h, g // 2)][:, g % 2, :],
+                        func=ACT.Identity, scale=gain, bias=shift,
+                    )
+                else:
+                    nc.vector.tensor_scalar(
+                        out=x_norm[:, h, g, :], in0=xt_banks[(h, g // 2)][:, g % 2, :],
+                        scalar1=gain, scalar2=shift, op0=ALU.mult, op1=ALU.add,
+                    )
+
+            x_grouped = head.tile([P, HALVES, PASSES, T_HALF, PACK], BF16, align_bytes=64)
+            x_codes = keep.tile([P, HALVES, PASSES, T_HALF], U32, align_bytes=64)
+            x_scales = keep.tile([P, HALVES, PASSES, T_HALF], U8, align_bytes=64)
+
+            def regroup_tokens(h):
+                for c in range(PASSES):
+                    regroup(
+                        nc.vector.tensor_copy,
+                        x_grouped[:, h, c, :, :],
+                        x_norm[:, h, c * PACK : (c + 1) * PACK, :],
+                    )
+
+            def quantise_tokens(h):
+                nc.vector.quantize_mx(
+                    out=x_codes[:, h, :, :].rearrange("p c n -> p (c n)").bitcast(FP8X4),
+                    scales=x_scales[:, h, :, :].rearrange("p c n -> p (c n)"),
+                    in_=x_grouped[:, h, :, :, :].rearrange("p c n t -> p (c n t)"),
+                )
 
             grouped = {}
             codes = {}
             accs = {}
             stages = {}
 
-            def gpsimd_copy(out, in_):
-                nc.gpsimd.tensor_scalar(
-                    out=out, in0=in_, scalar1=1.0, scalar2=0.0, op0=ALU.mult, op1=ALU.add
-                )
-
             def regroup_part(part):
                 w_grouped = grouped_pool.tile([P, PASSES, N_TILE, PACK], BF16, align_bytes=64)
-                first = (part % PARTS_PER_LOAD) * N_TILE
+                last = PASSES - 1
+                nc.gpsimd.tensor_scalar(
+                    out=w_grouped[:, last, 0:GPSIMD_COLS, :],
+                    in0=raw[part][last][:, :, 0:GPSIMD_COLS].rearrange("p t n -> p n t"),
+                    scalar1=1.0, scalar2=0.0, op0=ALU.mult, op1=ALU.add,
+                )
                 for c in range(PASSES):
-                    number = (part // PARTS_PER_LOAD) * PASSES + c
-                    if c == PASSES - 1 and part % GPSIMD_EVERY == 0:
-                        copy = gpsimd_copy
-                    else:
-                        copy = nc.scalar.copy
-                    regroup(copy, w_grouped[:, c, :, :], raw[number][:, :, first : first + N_TILE])
+                    start = GPSIMD_COLS if c == last else 0
+                    regroup(
+                        nc.scalar.copy, w_grouped[:, c, start:N_TILE, :], raw[part][c][:, :, start:N_TILE]
+                    )
                 grouped[part] = w_grouped
 
             def quantise_part(part):
@@ -225,18 +253,21 @@ def tile_stulayer_pa_kernel(tc, src, ln1_w, ln1_b, w_uvqk, b_uvqk, out):
                 codes[part] = (w_codes, w_scales)
 
             def multiply(part):
-                for i in range(TOKEN_TILES):
-                    acc_i = psum.tile([P, N_TILE], F32, name="acc_i", tag="bank")
-                    accs[(part, i)] = acc_i
                 w_codes, w_scales = codes[part]
-                for c in range(PASSES):
-                    columns = slice(c * N_TILE, (c + 1) * N_TILE)
-                    for i in range(TOKEN_TILES):
-                        tokens = slice(c * T + i * P, c * T + (i + 1) * P)
+                for i in range(TOKEN_TILES):
+                    h, local = divmod(i, TILES_PER_HALF)
+                    acc_i = psum.tile(
+                        [P, N_TILE], F32, name="acc_i",
+                        tag="bank%d" % ((part * TOKEN_TILES + i) % BANKS),
+                    )
+                    accs[(part, i)] = acc_i
+                    tokens = slice(local * P, (local + 1) * P)
+                    for c in range(PASSES):
+                        columns = slice(c * N_TILE, (c + 1) * N_TILE)
                         nc.tensor.matmul_mx(
-                            out=accs[(part, i)][:],
-                            lhsT=x_codes[:, tokens].bitcast(FP8X4),
-                            lhsT_scale=x_scales[:, tokens],
+                            out=acc_i[:],
+                            lhsT=x_codes[:, h, c, tokens].bitcast(FP8X4),
+                            lhsT_scale=x_scales[:, h, c, tokens],
                             rhs=w_codes[:, columns].bitcast(FP8X4),
                             rhs_scale=w_scales[:, columns],
                             start=(c == 0),
@@ -270,41 +301,40 @@ def tile_stulayer_pa_kernel(tc, src, ln1_w, ln1_b, w_uvqk, b_uvqk, out):
                             in_=stage[:],
                         )
 
+            statistics(0)
+            spread_bias(0)
+            spread_bias(1)
+            statistics(1)
+            turn_gain_and_shift()
+            normalise(0, nc.gpsimd)
+            spread_bias(2)
+            spread_bias(3)
+            turn_tokens(0)
+            statistics(2)
+            normalise(1, nc.gpsimd)
+            spread_bias(4)
+            spread_bias(5)
+            turn_tokens(1)
+            statistics(3)
+            normalise(2, nc.vector)
+            normalise(3, nc.vector)
+            spread_bias(6)
+            spread_bias(7)
+            turn_tokens(2)
+            turn_tokens(3)
+
             regroup_part(0)
-
-            x_norm = head.tile([P, GROUPS, T], BF16)
             for g in range(GROUPS):
-                c, t = divmod(g, PACK)
-                gain = gain_shift[:, t, c : c + 1]
-                shift = gain_shift[:, t, PASSES + c : PASSES + c + 1]
-                if g % 2 == 0:
-                    nc.scalar.activation(
-                        out=x_norm[:, g, :], in_=xt_banks[g][:], func=ACT.Identity,
-                        scale=gain, bias=shift,
-                    )
-                else:
-                    nc.vector.tensor_scalar(
-                        out=x_norm[:, g, :], in0=xt_banks[g][:], scalar1=gain, scalar2=shift,
-                        op0=ALU.mult, op1=ALU.add,
-                    )
-
-            x_grouped = head.tile([P, PASSES, T, PACK], BF16, align_bytes=64)
-            for c in range(PASSES):
-                regroup(
-                    nc.vector.tensor_copy,
-                    x_grouped[:, c, :, :],
-                    x_norm[:, c * PACK : (c + 1) * PACK, :],
-                )
+                gain_and_shift(0, g, False)
+            for g in range(GROUPS):
+                gain_and_shift(1, g, True)
+            regroup_tokens(0)
             quantise_part(0)
-            x_codes = keep.tile([P, PASSES * T], U32, align_bytes=64)
-            x_scales = keep.tile([P, PASSES * T], U8, align_bytes=64)
-            nc.vector.quantize_mx(
-                out=x_codes[:].bitcast(FP8X4),
-                scales=x_scales[:],
-                in_=x_grouped[:].rearrange("p c n t -> p (c n t)"),
-            )
+            quantise_tokens(0)
+            regroup_tokens(1)
+            quantise_tokens(1)
 
-        stage_pool = ctx.enter_context(tc.tile_pool(name="stage", bufs=3 * TOKEN_TILES))
+        stage_pool = ctx.enter_context(tc.tile_pool(name="stage", bufs=STAGES))
 
         for part in range(PARTS + 1):
             if 1 <= part < PARTS:
@@ -314,6 +344,3 @@ def tile_stulayer_pa_kernel(tc, src, ln1_w, ln1_b, w_uvqk, b_uvqk, out):
                 multiply(part)
             if part >= 1:
                 add_bias_and_store(part - 1)
-                loads_read = PASSES * (min(part + 1, PARTS) // PARTS_PER_LOAD)
-                if part % PARTS_PER_STORE == 0 and len(raw) < min(LOADS, LOADS_AHEAD + loads_read):
-                    load_w(len(raw), 0, 1)

@@ -26,13 +26,16 @@ T_HALF = T // HALVES
 BANKS = 8
 N_TILE = 512
 PARTS = N // N_TILE
-LOAD_PARTS = (1, 3, 4, 8)
+LOAD_PARTS = (2, 2, 4, 4, 4)
+LOADS_UP_FRONT = 8
 STORE_COLS = 1024
 STORES = N // STORE_COLS
 PARTS_PER_STORE = STORE_COLS // N_TILE
 STAGES = 13
 RUN = 4
 GPSIMD_COLS = 256
+GPSIMD_ALONE = 2
+WARM_UP = 6
 BN_FMAX = 512
 BN_STATS_DIM = 6
 BN_AGGR_DIM = 2
@@ -62,10 +65,12 @@ def tile_stulayer_pa_kernel(tc, src, ln1_w, ln1_b, w_uvqk, b_uvqk, out):
 
         with tc.tile_pool(name="head", bufs=1) as head:
 
-            ln_rows = keep.tile([P, P * PACK], BF16)
-            nc.vector.memset(ln_rows[:], 0.0)
+            zeros = keep.tile([P, N_TILE], BF16)
+            nc.vector.memset(zeros[:].bitcast(F32), 0.0)
             bias_rows = keep.tile([P, N_TILE], BF16)
-            nc.vector.memset(bias_rows[:], 0.0)
+            nc.vector.memset(bias_rows[:].bitcast(F32), 0.0)
+            ln_rows = keep.tile([P, P * PACK], BF16)
+            nc.vector.memset(ln_rows[:].bitcast(F32), 0.0)
             eps_col = keep.tile([P, 1], F32)
             nc.vector.memset(eps_col[:], EPS)
             x_tiles = []
@@ -73,7 +78,7 @@ def tile_stulayer_pa_kernel(tc, src, ln1_w, ln1_b, w_uvqk, b_uvqk, out):
                 x_i = head.tile([P, D], BF16, name="x%d" % i)
                 nc.sync.dma_start(out=x_i[:], in_=src_rows[i * P : (i + 1) * P, :])
                 x_tiles.append(x_i)
-                if i == 0:
+                if i == 1:
                     nc.sync.dma_start(
                         out=bias_rows[0:PARTS, :], in_=b_uvqk.rearrange("(r n) -> r n", n=N_TILE)
                     )
@@ -85,6 +90,7 @@ def tile_stulayer_pa_kernel(tc, src, ln1_w, ln1_b, w_uvqk, b_uvqk, out):
                         in_=ln1_b.rearrange("(c f) -> c f", c=PASSES),
                     )
             raw = []
+            loads = []
             first = 0
             for parts in LOAD_PARTS:
                 tiles = []
@@ -92,18 +98,24 @@ def tile_stulayer_pa_kernel(tc, src, ln1_w, ln1_b, w_uvqk, b_uvqk, out):
                     raw_tile = keep.tile(
                         [P, PACK, parts * N_TILE], BF16, name="raw%d_%d" % (first, c)
                     )
-                    nc.sync.dma_start(
-                        out=raw_tile[:], in_=w_view[:, c, :, first : first + parts * N_TILE]
-                    )
+                    loads.append((raw_tile, w_view[:, c, :, first : first + parts * N_TILE]))
                     tiles.append(raw_tile)
                 for j in range(parts):
                     raw.append([tile[:, :, j * N_TILE : (j + 1) * N_TILE] for tile in tiles])
                 first += parts * N_TILE
+            for raw_tile, source in loads[:LOADS_UP_FRONT]:
+                nc.sync.dma_start(out=raw_tile[:], in_=source)
 
             ident_bf = keep.tile([P, P], BF16)
             make_identity(nc, ident_bf[:])
             ident = keep.tile([P, P], F32)
             make_identity(nc, ident[:])
+
+            warm_ps = psum.tile([P, N_TILE], F32, tag="bank7")
+            for step in range(WARM_UP):
+                nc.tensor.matmul(
+                    out=warm_ps[:], lhsT=zeros[:, 0:P], rhs=zeros[:], start=True, stop=True
+                )
 
             gain_shift = keep.tile([P, PACK, 2 * PASSES], F32)
 
@@ -138,6 +150,10 @@ def tile_stulayer_pa_kernel(tc, src, ln1_w, ln1_b, w_uvqk, b_uvqk, out):
             mean_var = keep.tile([P, TOKEN_TILES, BN_AGGR_DIM], F32)
             std = keep.tile([P, TOKEN_TILES], F32)
             rstd = keep.tile([P, TOKEN_TILES], F32)
+            table_col = keep.tile([P, 1], F32)
+            nc.scalar.activation(
+                out=table_col[:], in_=eps_col[:], func=ACT.Sqrt, bias=eps_col[:, 0:1], scale=1.0
+            )
             neg_mean = keep.tile([P, TOKEN_TILES], F32)
             xhat_tiles = []
 
@@ -146,6 +162,8 @@ def tile_stulayer_pa_kernel(tc, src, ln1_w, ln1_b, w_uvqk, b_uvqk, out):
                     nc.vector.bn_stats(
                         out=stats[:, i, h, :], in_=x_tiles[i][:, h * BN_FMAX : (h + 1) * BN_FMAX]
                     )
+
+            def deviation(i):
                 nc.vector.bn_aggr(
                     out=mean_var[:, i, :], in_=stats[:, i, :, :].rearrange("p h s -> p (h s)")
                 )
@@ -153,22 +171,30 @@ def tile_stulayer_pa_kernel(tc, src, ln1_w, ln1_b, w_uvqk, b_uvqk, out):
                     out=std[:, i : i + 1], in_=mean_var[:, i, 1:2], func=ACT.Sqrt,
                     bias=eps_col[:, 0:1], scale=1.0,
                 )
-                nc.vector.tensor_scalar(
-                    out=neg_mean[:, i : i + 1], in0=mean_var[:, i, 0:1], scalar1=-1.0, scalar2=None,
-                    op0=ALU.mult,
-                )
 
-            def normalise(i, engine):
+            def invert(i):
                 nc.vector.reciprocal(out=rstd[:, i : i + 1], in_=std[:, i : i + 1])
+
+            def normalise(i, on_gpsimd):
                 xhat_i = head.tile([P, GROUPS, P], F32, name="xhat%d" % i)
-                engine.tensor_scalar(
-                    out=xhat_i[:].rearrange("p (c t) q -> p c t q", c=PASSES),
-                    in0=x_tiles[i][:].rearrange("p (c q t) -> p c t q", c=PASSES, t=PACK),
-                    scalar1=neg_mean[:, i : i + 1],
-                    scalar2=rstd[:, i : i + 1],
-                    op0=ALU.add,
-                    op1=ALU.mult,
-                )
+                xhat_view = xhat_i[:].rearrange("p (c t) q -> p c t q", c=PASSES)
+                x_view = x_tiles[i][:].rearrange("p (c q t) -> p c t q", c=PASSES, t=PACK)
+                if on_gpsimd:
+                    nc.gpsimd.tensor_scalar(
+                        out=neg_mean[:, i : i + 1], in0=mean_var[:, i, 0:1],
+                        scalar1=-1.0, scalar2=0.0, op0=ALU.mult, op1=ALU.add,
+                    )
+                    nc.gpsimd.tensor_scalar(
+                        out=xhat_view, in0=x_view,
+                        scalar1=neg_mean[:, i : i + 1], scalar2=rstd[:, i : i + 1],
+                        op0=ALU.add, op1=ALU.mult,
+                    )
+                else:
+                    nc.vector.tensor_scalar(
+                        out=xhat_view, in0=x_view,
+                        scalar1=mean_var[:, i, 0:1], scalar2=rstd[:, i : i + 1],
+                        op0=ALU.subtract, op1=ALU.mult,
+                    )
                 xhat_tiles.append(xhat_i)
 
             xt_banks = {}
@@ -228,18 +254,22 @@ def tile_stulayer_pa_kernel(tc, src, ln1_w, ln1_b, w_uvqk, b_uvqk, out):
             stages = {}
 
             def regroup_part(part):
+                gpsimd_cols = N_TILE if part < GPSIMD_ALONE else GPSIMD_COLS
                 w_grouped = grouped_pool.tile([P, PASSES, N_TILE, PACK], BF16, align_bytes=64)
                 last = PASSES - 1
                 nc.gpsimd.tensor_scalar(
-                    out=w_grouped[:, last, 0:GPSIMD_COLS, :],
-                    in0=raw[part][last][:, :, 0:GPSIMD_COLS].rearrange("p t n -> p n t"),
+                    out=w_grouped[:, last, 0:gpsimd_cols, :],
+                    in0=raw[part][last][:, :, 0:gpsimd_cols].rearrange("p t n -> p n t"),
                     scalar1=1.0, scalar2=0.0, op0=ALU.mult, op1=ALU.add,
                 )
                 for c in range(PASSES):
-                    start = GPSIMD_COLS if c == last else 0
-                    regroup(
-                        nc.scalar.copy, w_grouped[:, c, start:N_TILE, :], raw[part][c][:, :, start:N_TILE]
-                    )
+                    start = gpsimd_cols if c == last else 0
+                    if start < N_TILE:
+                        regroup(
+                            nc.scalar.copy,
+                            w_grouped[:, c, start:N_TILE, :],
+                            raw[part][c][:, :, start:N_TILE],
+                        )
                 grouped[part] = w_grouped
 
             def quantise_part(part):
@@ -274,11 +304,11 @@ def tile_stulayer_pa_kernel(tc, src, ln1_w, ln1_b, w_uvqk, b_uvqk, out):
                             stop=(c == PASSES - 1),
                         )
 
-            def add_bias_and_store(part):
+            def add_bias_and_store(part, tiles):
                 store = part // PARTS_PER_STORE
                 local = (part % PARTS_PER_STORE) * N_TILE
                 first = part * N_TILE
-                for i in range(TOKEN_TILES):
+                for i in tiles:
                     if local == 0:
                         stage_i = stage_pool.tile([P, STORE_COLS], F32, name="stage_i", tag="stage")
                         stages[(store, i)] = stage_i
@@ -302,34 +332,42 @@ def tile_stulayer_pa_kernel(tc, src, ln1_w, ln1_b, w_uvqk, b_uvqk, out):
                         )
 
             statistics(0)
-            spread_bias(0)
-            spread_bias(1)
+            deviation(0)
             statistics(1)
-            turn_gain_and_shift()
-            normalise(0, nc.gpsimd)
+            spread_bias(0)
+            invert(0)
+            normalise(0, True)
+            deviation(1)
+            spread_bias(1)
             spread_bias(2)
-            spread_bias(3)
-            turn_tokens(0)
             statistics(2)
-            normalise(1, nc.gpsimd)
-            spread_bias(4)
-            spread_bias(5)
-            turn_tokens(1)
+            invert(1)
+            normalise(1, True)
+            turn_gain_and_shift()
+            spread_bias(3)
+            deviation(2)
             statistics(3)
-            normalise(2, nc.vector)
-            normalise(3, nc.vector)
+            spread_bias(4)
+            invert(2)
+            deviation(3)
+            spread_bias(5)
+            turn_tokens(0)
+            normalise(2, False)
+            invert(3)
+            normalise(3, False)
             spread_bias(6)
             spread_bias(7)
+            turn_tokens(1)
             turn_tokens(2)
             turn_tokens(3)
 
             regroup_part(0)
             for g in range(GROUPS):
-                gain_and_shift(0, g, False)
+                gain_and_shift(0, g, g >= GROUPS - 2)
             for g in range(GROUPS):
                 gain_and_shift(1, g, True)
-            regroup_tokens(0)
             quantise_part(0)
+            regroup_tokens(0)
             quantise_tokens(0)
             regroup_tokens(1)
             quantise_tokens(1)
@@ -337,10 +375,16 @@ def tile_stulayer_pa_kernel(tc, src, ln1_w, ln1_b, w_uvqk, b_uvqk, out):
         stage_pool = ctx.enter_context(tc.tile_pool(name="stage", bufs=STAGES))
 
         for part in range(PARTS + 1):
+            if part >= 1:
+                add_bias_and_store(part - 1, range(1))
             if 1 <= part < PARTS:
                 regroup_part(part)
                 quantise_part(part)
             if part < PARTS:
                 multiply(part)
             if part >= 1:
-                add_bias_and_store(part - 1)
+                add_bias_and_store(part - 1, range(1, TOKEN_TILES))
+                load = LOADS_UP_FRONT + part // PARTS_PER_STORE - 1
+                if part % PARTS_PER_STORE == 0 and load < len(loads):
+                    raw_tile, source = loads[load]
+                    nc.sync.dma_start(out=raw_tile[:], in_=source)

@@ -34,7 +34,6 @@ PARTS_PER_STORE = STORE_COLS // N_TILE
 STAGES = 13
 RUN = 4
 GPSIMD_COLS = 256
-GPSIMD_ALONE = 2
 WARM_UP = 6
 BN_FMAX = 512
 BN_STATS_DIM = 6
@@ -129,9 +128,9 @@ def tile_stulayer_pa_kernel(tc, src, ln1_w, ln1_b, w_uvqk, b_uvqk, out):
 
             bias_all = keep.tile([P, N], BF16)
 
-            def spread_bias(pair):
+            def spread_bias(pair, bank):
                 bias_ps = psum.tile(
-                    [P, 2 * N_TILE], BF16, name="bias_ps", tag="bank%d" % (BANKS // 2 + pair % (BANKS // 2))
+                    [P, 2 * N_TILE], BF16, name="bias_ps", tag="bank%d" % bank
                 )
                 for half in range(2):
                     r = 2 * pair + half
@@ -254,13 +253,14 @@ def tile_stulayer_pa_kernel(tc, src, ln1_w, ln1_b, w_uvqk, b_uvqk, out):
             stages = {}
 
             def regroup_part(part):
-                gpsimd_cols = N_TILE if part < GPSIMD_ALONE else GPSIMD_COLS
+                gpsimd_cols = N_TILE if part == 0 else GPSIMD_COLS
                 w_grouped = grouped_pool.tile([P, PASSES, N_TILE, PACK], BF16, align_bytes=64)
                 last = PASSES - 1
                 nc.gpsimd.tensor_scalar(
                     out=w_grouped[:, last, 0:gpsimd_cols, :],
                     in0=raw[part][last][:, :, 0:gpsimd_cols].rearrange("p t n -> p n t"),
-                    scalar1=1.0, scalar2=0.0, op0=ALU.mult, op1=ALU.add,
+                    scalar1=one_col[:, 0:1] if part == 1 else 1.0, scalar2=0.0,
+                    op0=ALU.mult, op1=ALU.add,
                 )
                 for c in range(PASSES):
                     start = gpsimd_cols if c == last else 0
@@ -334,56 +334,58 @@ def tile_stulayer_pa_kernel(tc, src, ln1_w, ln1_b, w_uvqk, b_uvqk, out):
             statistics(0)
             deviation(0)
             statistics(1)
-            spread_bias(0)
+            spread_bias(0, 4)
             invert(0)
             normalise(0, True)
             deviation(1)
-            spread_bias(1)
-            spread_bias(2)
+            spread_bias(1, 5)
+            spread_bias(2, 6)
             statistics(2)
             invert(1)
             normalise(1, True)
             turn_gain_and_shift()
-            spread_bias(3)
+            spread_bias(3, 7)
             deviation(2)
             statistics(3)
-            spread_bias(4)
+            spread_bias(4, 4)
             invert(2)
             deviation(3)
-            spread_bias(5)
+            spread_bias(5, 5)
             turn_tokens(0)
             normalise(2, False)
             invert(3)
             normalise(3, False)
-            spread_bias(6)
-            spread_bias(7)
             turn_tokens(1)
             turn_tokens(2)
             turn_tokens(3)
 
             regroup_part(0)
-            for g in range(GROUPS):
-                gain_and_shift(0, g, g >= GROUPS - 2)
-            for g in range(GROUPS):
-                gain_and_shift(1, g, True)
+            for h in range(HALVES):
+                for g in range(GROUPS):
+                    gain_and_shift(h, g, h == 1)
+            spread_bias(6, 2)
+            spread_bias(7, 3)
             quantise_part(0)
-            regroup_tokens(0)
-            quantise_tokens(0)
-            regroup_tokens(1)
-            quantise_tokens(1)
+            for h in range(HALVES):
+                regroup_tokens(h)
+            for h in range(HALVES):
+                quantise_tokens(h)
+            one_col = keep.tile([P, 1], F32)
+            nc.vector.memset(one_col[:], 1.0)
 
         stage_pool = ctx.enter_context(tc.tile_pool(name="stage", bufs=STAGES))
 
         for part in range(PARTS + 1):
+            ahead = TOKEN_TILES - 1 if part == 1 else 1
             if part >= 1:
-                add_bias_and_store(part - 1, range(1))
+                add_bias_and_store(part - 1, range(ahead))
             if 1 <= part < PARTS:
                 regroup_part(part)
                 quantise_part(part)
             if part < PARTS:
                 multiply(part)
             if part >= 1:
-                add_bias_and_store(part - 1, range(1, TOKEN_TILES))
+                add_bias_and_store(part - 1, range(ahead, TOKEN_TILES))
                 load = LOADS_UP_FRONT + part // PARTS_PER_STORE - 1
                 if part % PARTS_PER_STORE == 0 and load < len(loads):
                     raw_tile, source = loads[load]

@@ -26,12 +26,10 @@ T_HALF = T // HALVES
 BANKS = 8
 N_TILE = 512
 PARTS = N // N_TILE
-LOAD_PARTS = (2, 2, 4, 4, 4)
-LOADS_UP_FRONT = 8
-STORE_COLS = 1024
-STORES = N // STORE_COLS
-PARTS_PER_STORE = STORE_COLS // N_TILE
-STAGES = 13
+CHUNK_PARTS = 4
+CHUNKS = PARTS // CHUNK_PARTS
+CHUNKS_HELD = 3
+STORE_PARTS = (4, 4, 4, 2, 2)
 RUN = 4
 GPSIMD_COLS = 256
 WARM_UP = 6
@@ -58,6 +56,7 @@ def tile_stulayer_pa_kernel(tc, src, ln1_w, ln1_b, w_uvqk, b_uvqk, out):
     with ExitStack() as ctx:
         keep = ctx.enter_context(tc.tile_pool(name="keep", bufs=1))
         grouped_pool = ctx.enter_context(tc.tile_pool(name="grouped", bufs=2))
+        raw_pool = ctx.enter_context(tc.tile_pool(name="raw", bufs=CHUNKS_HELD))
         code_pool = ctx.enter_context(tc.tile_pool(name="codes", bufs=3))
         psum = ctx.enter_context(tc.psum_pool(name="psum", bufs=1))
         ctx.enter_context(tc.manual_schedule())
@@ -88,22 +87,25 @@ def tile_stulayer_pa_kernel(tc, src, ln1_w, ln1_b, w_uvqk, b_uvqk, out):
                         out=ln_rows[PASSES : 2 * PASSES, :],
                         in_=ln1_b.rearrange("(c f) -> c f", c=PASSES),
                     )
-            raw = []
-            loads = []
-            first = 0
-            for parts in LOAD_PARTS:
-                tiles = []
-                for c in range(PASSES):
-                    raw_tile = keep.tile(
-                        [P, PACK, parts * N_TILE], BF16, name="raw%d_%d" % (first, c)
+            raw = {}
+
+            def load_w(chunk, c, pieces):
+                width = CHUNK_PARTS * N_TILE // pieces
+                raw_tile = raw_pool.tile(
+                    [P, PACK, CHUNK_PARTS * N_TILE], BF16, name="raw_tile", tag="pass%d" % c
+                )
+                raw[(chunk, c)] = raw_tile
+                for piece in range(pieces):
+                    local = piece * width
+                    first = chunk * CHUNK_PARTS * N_TILE + local
+                    nc.sync.dma_start(
+                        out=raw_tile[:, :, local : local + width],
+                        in_=w_view[:, c, :, first : first + width],
                     )
-                    loads.append((raw_tile, w_view[:, c, :, first : first + parts * N_TILE]))
-                    tiles.append(raw_tile)
-                for j in range(parts):
-                    raw.append([tile[:, :, j * N_TILE : (j + 1) * N_TILE] for tile in tiles])
-                first += parts * N_TILE
-            for raw_tile, source in loads[:LOADS_UP_FRONT]:
-                nc.sync.dma_start(out=raw_tile[:], in_=source)
+
+            for chunk in range(CHUNKS_HELD):
+                for c in range(PASSES):
+                    load_w(chunk, c, 2 if chunk == 0 and c == PASSES - 1 else 1)
 
             ident_bf = keep.tile([P, P], BF16)
             make_identity(nc, ident_bf[:])
@@ -256,9 +258,12 @@ def tile_stulayer_pa_kernel(tc, src, ln1_w, ln1_b, w_uvqk, b_uvqk, out):
                 gpsimd_cols = N_TILE if part == 0 else GPSIMD_COLS
                 w_grouped = grouped_pool.tile([P, PASSES, N_TILE, PACK], BF16, align_bytes=64)
                 last = PASSES - 1
+                chunk, local = divmod(part, CHUNK_PARTS)
+                columns = slice(local * N_TILE, (local + 1) * N_TILE)
+                rows = [raw[(chunk, c)][:, :, columns] for c in range(PASSES)]
                 nc.gpsimd.tensor_scalar(
                     out=w_grouped[:, last, 0:gpsimd_cols, :],
-                    in0=raw[part][last][:, :, 0:gpsimd_cols].rearrange("p t n -> p n t"),
+                    in0=rows[last][:, :, 0:gpsimd_cols].rearrange("p t n -> p n t"),
                     scalar1=one_col[:, 0:1] if part == 1 else 1.0, scalar2=0.0,
                     op0=ALU.mult, op1=ALU.add,
                 )
@@ -268,7 +273,7 @@ def tile_stulayer_pa_kernel(tc, src, ln1_w, ln1_b, w_uvqk, b_uvqk, out):
                         regroup(
                             nc.scalar.copy,
                             w_grouped[:, c, start:N_TILE, :],
-                            raw[part][c][:, :, start:N_TILE],
+                            rows[c][:, :, start:N_TILE],
                         )
                 grouped[part] = w_grouped
 
@@ -304,30 +309,32 @@ def tile_stulayer_pa_kernel(tc, src, ln1_w, ln1_b, w_uvqk, b_uvqk, out):
                             stop=(c == PASSES - 1),
                         )
 
+            group_of = []
+            for group, parts in enumerate(STORE_PARTS):
+                group_of.extend([(group, local) for local in range(parts)])
+
             def add_bias_and_store(part, tiles):
-                store = part // PARTS_PER_STORE
-                local = (part % PARTS_PER_STORE) * N_TILE
-                first = part * N_TILE
+                group, local = group_of[part]
+                parts = STORE_PARTS[group]
                 for i in tiles:
                     if local == 0:
-                        stage_i = stage_pool.tile([P, STORE_COLS], F32, name="stage_i", tag="stage")
-                        stages[(store, i)] = stage_i
-                    stage = stages[(store, i)]
-                    token_rows = slice(i * P, (i + 1) * P)
+                        set_name = "narrow" if group == len(STORE_PARTS) - 2 else "wide"
+                        stages[i] = stage_pool.tile(
+                            [P, parts * N_TILE], F32, name="stage_i", tag="%s%d" % (set_name, i),
+                            bufs=1 if set_name == "narrow" else 2,
+                        )
+                    stage = stages[i]
                     nc.vector.tensor_tensor(
-                        out=stage[:, local : local + N_TILE],
+                        out=stage[:, local * N_TILE : (local + 1) * N_TILE],
                         in0=accs[(part, i)][:],
-                        in1=bias_all[:, first : first + N_TILE],
+                        in1=bias_all[:, part * N_TILE : (part + 1) * N_TILE],
                         op=ALU.add,
                     )
-                    if store == STORES - 1:
+                    if local == parts - 1:
                         nc.sync.dma_start(
-                            out=out_rows[token_rows, first : first + N_TILE],
-                            in_=stage[:, local : local + N_TILE],
-                        )
-                    elif local + N_TILE == STORE_COLS:
-                        nc.sync.dma_start(
-                            out=out_rows[token_rows, store * STORE_COLS : (store + 1) * STORE_COLS],
+                            out=out_rows[
+                                i * P : (i + 1) * P, (part - local) * N_TILE : (part + 1) * N_TILE
+                            ],
                             in_=stage[:],
                         )
 
@@ -373,7 +380,7 @@ def tile_stulayer_pa_kernel(tc, src, ln1_w, ln1_b, w_uvqk, b_uvqk, out):
             one_col = keep.tile([P, 1], F32)
             nc.vector.memset(one_col[:], 1.0)
 
-        stage_pool = ctx.enter_context(tc.tile_pool(name="stage", bufs=STAGES))
+        stage_pool = ctx.enter_context(tc.tile_pool(name="stage", bufs=2))
 
         for part in range(PARTS + 1):
             ahead = TOKEN_TILES - 1 if part == 1 else 1
@@ -386,7 +393,7 @@ def tile_stulayer_pa_kernel(tc, src, ln1_w, ln1_b, w_uvqk, b_uvqk, out):
                 multiply(part)
             if part >= 1:
                 add_bias_and_store(part - 1, range(ahead, TOKEN_TILES))
-                load = LOADS_UP_FRONT + part // PARTS_PER_STORE - 1
-                if part % PARTS_PER_STORE == 0 and load < len(loads):
-                    raw_tile, source = loads[load]
-                    nc.sync.dma_start(out=raw_tile[:], in_=source)
+                if part == STORE_PARTS[0]:
+                    for chunk in range(CHUNKS_HELD, CHUNKS):
+                        for c in range(PASSES):
+                            load_w(chunk, c, 1)

from contextlib import ExitStack

import concourse.mybir as mybir
from concourse.masks import make_identity

F32 = mybir.dt.float32
BF16 = mybir.dt.bfloat16
U32 = mybir.dt.uint32
U8 = mybir.dt.uint8
FP8X4 = mybir.dt.float8_e4m3fn_x4
ALU = mybir.AluOpType
ACT = mybir.ActivationFunctionType

P = 128
PACK = 4
T = 512
D = 1024
N = 8192
EPS = 1e-5
PASSES = D // (P * PACK)
GROUPS = PASSES * PACK
TOKEN_TILES = T // P
HALVES = 2
TILES_PER_HALF = TOKEN_TILES // HALVES
T_HALF = T // HALVES
BANKS = 8
N_TILE = 512
PARTS = N // N_TILE
CHUNK_PARTS = 4
CHUNKS = PARTS // CHUNK_PARTS
CHUNKS_HELD = 3
STORE_PARTS = (4, 4, 4, 2, 2)
RUN = 4
GPSIMD_COLS = 256
WARM_UP = 6
BN_FMAX = 512
BN_STATS_DIM = 6
BN_AGGR_DIM = 2

FLOPS = 2 * T * D * N


def regroup(engine_copy, grouped, rows):
    engine_copy(
        out=grouped.rearrange("p (q i) t -> p q t i", i=RUN),
        in_=rows.rearrange("p t (q i) -> p q t i", i=RUN),
    )


def tile_stulayer_pa_kernel(tc, src, ln1_w, ln1_b, w_uvqk, b_uvqk, out):
    nc = tc.nc
    src_rows = src.rearrange("t b d -> (t b) d")
    out_rows = out.rearrange("t b n -> (t b) n")
    w_view = w_uvqk.rearrange("(c p t) n -> p c t n", c=PASSES, t=PACK, p=P)

    with ExitStack() as ctx:
        keep = ctx.enter_context(tc.tile_pool(name="keep", bufs=1))
        grouped_pool = ctx.enter_context(tc.tile_pool(name="grouped", bufs=2))
        raw_pool = ctx.enter_context(tc.tile_pool(name="raw", bufs=CHUNKS_HELD))
        code_pool = ctx.enter_context(tc.tile_pool(name="codes", bufs=3))
        psum = ctx.enter_context(tc.psum_pool(name="psum", bufs=1))
        ctx.enter_context(tc.manual_schedule())

        with tc.tile_pool(name="head", bufs=1) as head:

            zeros = keep.tile([P, N_TILE], BF16)
            nc.vector.memset(zeros[:].bitcast(F32), 0.0)
            bias_rows = keep.tile([P, N_TILE], BF16)
            nc.vector.memset(bias_rows[:].bitcast(F32), 0.0)
            ln_rows = keep.tile([P, P * PACK], BF16)
            nc.vector.memset(ln_rows[:].bitcast(F32), 0.0)
            eps_col = keep.tile([P, 1], F32)
            nc.vector.memset(eps_col[:], EPS)
            x_tiles = []
            for i in range(TOKEN_TILES):
                x_i = head.tile([P, D], BF16, name="x%d" % i)
                nc.sync.dma_start(out=x_i[:], in_=src_rows[i * P : (i + 1) * P, :])
                x_tiles.append(x_i)
                if i == 1:
                    nc.sync.dma_start(
                        out=bias_rows[0:PARTS, :], in_=b_uvqk.rearrange("(r n) -> r n", n=N_TILE)
                    )
                    nc.sync.dma_start(
                        out=ln_rows[0:PASSES, :], in_=ln1_w.rearrange("(c f) -> c f", c=PASSES)
                    )
                    nc.sync.dma_start(
                        out=ln_rows[PASSES : 2 * PASSES, :],
                        in_=ln1_b.rearrange("(c f) -> c f", c=PASSES),
                    )
            raw = {}

            def load_w(chunk, c, pieces):
                width = CHUNK_PARTS * N_TILE // pieces
                raw_tile = raw_pool.tile(
                    [P, PACK, CHUNK_PARTS * N_TILE], BF16, name="raw_tile", tag="pass%d" % c
                )
                raw[(chunk, c)] = raw_tile
                for piece in range(pieces):
                    local = piece * width
                    first = chunk * CHUNK_PARTS * N_TILE + local
                    nc.sync.dma_start(
                        out=raw_tile[:, :, local : local + width],
                        in_=w_view[:, c, :, first : first + width],
                    )

            for chunk in range(CHUNKS_HELD):
                for c in range(PASSES):
                    load_w(chunk, c, 2 if chunk == 0 and c == PASSES - 1 else 1)

            ident_bf = keep.tile([P, P], BF16)
            make_identity(nc, ident_bf[:])
            ident = keep.tile([P, P], F32)
            make_identity(nc, ident[:])

            warm_ps = psum.tile([P, N_TILE], F32, tag="bank7")
            for step in range(WARM_UP):
                nc.tensor.matmul(
                    out=warm_ps[:], lhsT=zeros[:, 0:P], rhs=zeros[:], start=True, stop=True
                )

            gain_shift = keep.tile([P, PACK, 2 * PASSES], F32)

            def turn_gain_and_shift():
                ln_cols_ps = psum.tile([P, PACK, P], BF16, tag="bank0")
                for t in range(PACK):
                    nc.tensor.transpose(
                        ln_cols_ps[:, t, :], ln_rows[:, t : P * PACK : PACK], ident_bf[:]
                    )
                nc.vector.tensor_copy(out=gain_shift[:], in_=ln_cols_ps[:, :, 0 : 2 * PASSES])

            bias_all = keep.tile([P, N], BF16)

            def spread_bias(pair, bank):
                bias_ps = psum.tile(
                    [P, 2 * N_TILE], BF16, name="bias_ps", tag="bank%d" % bank
                )
                for half in range(2):
                    r = 2 * pair + half
                    nc.tensor.matmul(
                        out=bias_ps[:, half * N_TILE : (half + 1) * N_TILE],
                        lhsT=ident_bf[:, r : r + 1].to_broadcast([P, P]),
                        rhs=bias_rows[:],
                        start=True,
                        stop=True,
                    )
                nc.scalar.copy(
                    out=bias_all[:, pair * 2 * N_TILE : (pair + 1) * 2 * N_TILE], in_=bias_ps[:]
                )

            stats = keep.tile([P, TOKEN_TILES, D // BN_FMAX, BN_STATS_DIM], F32)
            mean_var = keep.tile([P, TOKEN_TILES, BN_AGGR_DIM], F32)
            std = keep.tile([P, TOKEN_TILES], F32)
            rstd = keep.tile([P, TOKEN_TILES], F32)
            table_col = keep.tile([P, 1], F32)
            nc.scalar.activation(
                out=table_col[:], in_=eps_col[:], func=ACT.Sqrt, bias=eps_col[:, 0:1], scale=1.0
            )
            neg_mean = keep.tile([P, TOKEN_TILES], F32)
            xhat_tiles = []

            def statistics(i):
                for h in range(D // BN_FMAX):
                    nc.vector.bn_stats(
                        out=stats[:, i, h, :], in_=x_tiles[i][:, h * BN_FMAX : (h + 1) * BN_FMAX]
                    )

            def deviation(i):
                nc.vector.bn_aggr(
                    out=mean_var[:, i, :], in_=stats[:, i, :, :].rearrange("p h s -> p (h s)")
                )
                nc.scalar.activation(
                    out=std[:, i : i + 1], in_=mean_var[:, i, 1:2], func=ACT.Sqrt,
                    bias=eps_col[:, 0:1], scale=1.0,
                )

            def invert(i):
                nc.vector.reciprocal(out=rstd[:, i : i + 1], in_=std[:, i : i + 1])

            def normalise(i, on_gpsimd):
                xhat_i = head.tile([P, GROUPS, P], F32, name="xhat%d" % i)
                xhat_view = xhat_i[:].rearrange("p (c t) q -> p c t q", c=PASSES)
                x_view = x_tiles[i][:].rearrange("p (c q t) -> p c t q", c=PASSES, t=PACK)
                if on_gpsimd:
                    nc.gpsimd.tensor_scalar(
                        out=neg_mean[:, i : i + 1], in0=mean_var[:, i, 0:1],
                        scalar1=-1.0, scalar2=0.0, op0=ALU.mult, op1=ALU.add,
                    )
                    nc.gpsimd.tensor_scalar(
                        out=xhat_view, in0=x_view,
                        scalar1=neg_mean[:, i : i + 1], scalar2=rstd[:, i : i + 1],
                        op0=ALU.add, op1=ALU.mult,
                    )
                else:
                    nc.vector.tensor_scalar(
                        out=xhat_view, in0=x_view,
                        scalar1=mean_var[:, i, 0:1], scalar2=rstd[:, i : i + 1],
                        op0=ALU.subtract, op1=ALU.mult,
                    )
                xhat_tiles.append(xhat_i)

            xt_banks = {}

            def turn_tokens(i):
                h, local = divmod(i, TILES_PER_HALF)
                for g in range(GROUPS):
                    if local == 0 and g % 2 == 0:
                        xt_banks[(h, g // 2)] = psum.tile(
                            [P, 2, T_HALF], F32, name="xt", tag="bank%d" % (h * (BANKS // 2) + g // 2)
                        )
                    nc.tensor.transpose(
                        xt_banks[(h, g // 2)][:, g % 2, local * P : (local + 1) * P],
                        xhat_tiles[i][:, g, :],
                        ident[:],
                    )

            x_norm = head.tile([P, HALVES, GROUPS, T_HALF], BF16)

            def gain_and_shift(h, g, on_scalar):
                c, t = divmod(g, PACK)
                gain = gain_shift[:, t, c : c + 1]
                shift = gain_shift[:, t, PASSES + c : PASSES + c + 1]
                if on_scalar:
                    nc.scalar.activation(
                        out=x_norm[:, h, g, :], in_=xt_banks[(h, g // 2)][:, g % 2, :],
                        func=ACT.Identity, scale=gain, bias=shift,
                    )
                else:
                    nc.vector.tensor_scalar(
                        out=x_norm[:, h, g, :], in0=xt_banks[(h, g // 2)][:, g % 2, :],
                        scalar1=gain, scalar2=shift, op0=ALU.mult, op1=ALU.add,
                    )

            x_grouped = head.tile([P, HALVES, PASSES, T_HALF, PACK], BF16, align_bytes=64)
            x_codes = keep.tile([P, HALVES, PASSES, T_HALF], U32, align_bytes=64)
            x_scales = keep.tile([P, HALVES, PASSES, T_HALF], U8, align_bytes=64)

            def regroup_tokens(h):
                for c in range(PASSES):
                    regroup(
                        nc.vector.tensor_copy,
                        x_grouped[:, h, c, :, :],
                        x_norm[:, h, c * PACK : (c + 1) * PACK, :],
                    )

            def quantise_tokens(h):
                nc.vector.quantize_mx(
                    out=x_codes[:, h, :, :].rearrange("p c n -> p (c n)").bitcast(FP8X4),
                    scales=x_scales[:, h, :, :].rearrange("p c n -> p (c n)"),
                    in_=x_grouped[:, h, :, :, :].rearrange("p c n t -> p (c n t)"),
                )

            grouped = {}
            codes = {}
            accs = {}
            stages = {}

            def regroup_part(part):
                gpsimd_cols = N_TILE if part == 0 else GPSIMD_COLS
                w_grouped = grouped_pool.tile([P, PASSES, N_TILE, PACK], BF16, align_bytes=64)
                last = PASSES - 1
                chunk, local = divmod(part, CHUNK_PARTS)
                columns = slice(local * N_TILE, (local + 1) * N_TILE)
                rows = [raw[(chunk, c)][:, :, columns] for c in range(PASSES)]
                nc.gpsimd.tensor_scalar(
                    out=w_grouped[:, last, 0:gpsimd_cols, :],
                    in0=rows[last][:, :, 0:gpsimd_cols].rearrange("p t n -> p n t"),
                    scalar1=one_col[:, 0:1] if part == 1 else 1.0, scalar2=0.0,
                    op0=ALU.mult, op1=ALU.add,
                )
                for c in range(PASSES):
                    start = gpsimd_cols if c == last else 0
                    if start < N_TILE:
                        regroup(
                            nc.scalar.copy,
                            w_grouped[:, c, start:N_TILE, :],
                            rows[c][:, :, start:N_TILE],
                        )
                grouped[part] = w_grouped

            def quantise_part(part):
                w_codes = code_pool.tile([P, PASSES * N_TILE], U32, align_bytes=64)
                w_scales = code_pool.tile([P, PASSES * N_TILE], U8, align_bytes=64)
                nc.vector.quantize_mx(
                    out=w_codes[:].bitcast(FP8X4),
                    scales=w_scales[:],
                    in_=grouped[part][:].rearrange("p c n t -> p (c n t)"),
                )
                codes[part] = (w_codes, w_scales)

            def multiply(part):
                w_codes, w_scales = codes[part]
                for i in range(TOKEN_TILES):
                    h, local = divmod(i, TILES_PER_HALF)
                    acc_i = psum.tile(
                        [P, N_TILE], F32, name="acc_i",
                        tag="bank%d" % ((part * TOKEN_TILES + i) % BANKS),
                    )
                    accs[(part, i)] = acc_i
                    tokens = slice(local * P, (local + 1) * P)
                    for c in range(PASSES):
                        columns = slice(c * N_TILE, (c + 1) * N_TILE)
                        nc.tensor.matmul_mx(
                            out=acc_i[:],
                            lhsT=x_codes[:, h, c, tokens].bitcast(FP8X4),
                            lhsT_scale=x_scales[:, h, c, tokens],
                            rhs=w_codes[:, columns].bitcast(FP8X4),
                            rhs_scale=w_scales[:, columns],
                            start=(c == 0),
                            stop=(c == PASSES - 1),
                        )

            group_of = []
            for group, parts in enumerate(STORE_PARTS):
                group_of.extend([(group, local) for local in range(parts)])

            def add_bias_and_store(part, tiles):
                group, local = group_of[part]
                parts = STORE_PARTS[group]
                for i in tiles:
                    if local == 0:
                        set_name = "narrow" if group == len(STORE_PARTS) - 2 else "wide"
                        stages[i] = stage_pool.tile(
                            [P, parts * N_TILE], F32, name="stage_i", tag="%s%d" % (set_name, i),
                            bufs=1 if set_name == "narrow" else 2,
                        )
                    stage = stages[i]
                    nc.vector.tensor_tensor(
                        out=stage[:, local * N_TILE : (local + 1) * N_TILE],
                        in0=accs[(part, i)][:],
                        in1=bias_all[:, part * N_TILE : (part + 1) * N_TILE],
                        op=ALU.add,
                    )
                    if local == parts - 1:
                        nc.sync.dma_start(
                            out=out_rows[
                                i * P : (i + 1) * P, (part - local) * N_TILE : (part + 1) * N_TILE
                            ],
                            in_=stage[:],
                        )

            statistics(0)
            deviation(0)
            statistics(1)
            spread_bias(0, 4)
            invert(0)
            normalise(0, True)
            deviation(1)
            spread_bias(1, 5)
            spread_bias(2, 6)
            statistics(2)
            invert(1)
            normalise(1, True)
            turn_gain_and_shift()
            spread_bias(3, 7)
            deviation(2)
            statistics(3)
            spread_bias(4, 4)
            invert(2)
            deviation(3)
            spread_bias(5, 5)
            turn_tokens(0)
            normalise(2, False)
            invert(3)
            normalise(3, False)
            turn_tokens(1)
            turn_tokens(2)
            turn_tokens(3)

            regroup_part(0)
            for h in range(HALVES):
                for g in range(GROUPS):
                    gain_and_shift(h, g, h == 1)
            spread_bias(6, 2)
            spread_bias(7, 3)
            quantise_part(0)
            for h in range(HALVES):
                regroup_tokens(h)
            for h in range(HALVES):
                quantise_tokens(h)
            one_col = keep.tile([P, 1], F32)
            nc.vector.memset(one_col[:], 1.0)

        stage_pool = ctx.enter_context(tc.tile_pool(name="stage", bufs=2))

        for part in range(PARTS + 1):
            ahead = TOKEN_TILES - 1 if part == 1 else 1
            if part >= 1:
                add_bias_and_store(part - 1, range(ahead))
            if 1 <= part < PARTS:
                regroup_part(part)
                quantise_part(part)
            if part < PARTS:
                multiply(part)
            if part >= 1:
                add_bias_and_store(part - 1, range(ahead, TOKEN_TILES))
                if part == STORE_PARTS[0]:
                    for chunk in range(CHUNKS_HELD, CHUNKS):
                        for c in range(PASSES):
                            load_w(chunk, c, 1)
